import numpy as np
import ml_dtypes


def mxq(x, axis, fmt="e4m3"):
    dtype, down = {"e4m3": (ml_dtypes.float8_e4m3fn, 7), "e5m2": (ml_dtypes.float8_e5m2, 14)}[fmt]
    v = np.moveaxis(np.asarray(x, np.float32).astype(ml_dtypes.bfloat16).astype(np.float64), axis, -1)
    blocks = v.reshape(v.shape[:-1] + (-1, 32))
    amax = np.abs(blocks).max(-1, keepdims=True)
    byte = np.maximum(np.where(amax > 0, np.frexp(amax)[1] - 1 + 127, 0) - down, 1)
    scale = np.exp2(byte - 127.0)
    codes = (blocks / scale).astype(np.float32).astype(dtype).astype(np.float64)
    return np.moveaxis((codes * scale).reshape(v.shape), -1, axis)


WIDE = False


def mx_kscale(k):
    if not WIDE:
        return np.ones(k)
    levels = np.array([10, -10, 5, -5, 0])
    if k % 512:
        return np.exp2(np.random.permutation(np.resize(levels, k // 32))).repeat(32)
    a = np.empty((k // 512, 16))
    for p in range(k // 512):
        a[p, :8] = np.random.permutation(np.resize(levels, 8))
        for g in range(8):
            far = levels[np.abs(levels - a[p, g]) >= 10]
            a[p, g + 8] = far[np.random.randint(len(far))]
    return np.exp2(a.ravel()).repeat(32)


BF16 = ml_dtypes.bfloat16


def bf(x):
    return np.asarray(x, np.float32).astype(BF16)


def f64(x):
    return np.asarray(x).astype(np.float64)


B, IN_C, OUT_C, H, W, K, STRIDE, PAD = 512, 512, 128, 4, 4, 3, 1, 1
OH = (H + 2 * PAD - K) // STRIDE + 1
OW = (W + 2 * PAD - K) // STRIDE + 1


def _span(t, n_in, n_out):
    lo = max(0, -((t - PAD) // STRIDE))
    hi = min(n_out, (n_in - 1 + PAD - t) // STRIDE + 1)
    return lo, hi


def setup_inputs():
    s = mx_kscale(IN_C)
    x = np.random.standard_normal((B, IN_C, H, W)) * s[None, :, None, None]
    weights = np.random.uniform(0.0, 1.0, (OH, OW, OUT_C, IN_C, K, K)) * (1.7 / np.sqrt(IN_C * K * K)) / s[None, None, None, :, None, None]
    bias = np.random.uniform(0.0, 1.0, (OUT_C, OH, OW))
    return {"x": bf(x), "weights": bf(weights), "bias": bf(bias)}


def reference(x, weights, bias):
    xq = mxq(f64(x), 1, "e4m3")
    wf = f64(weights)
    acc = np.zeros((OH, OW, B, OUT_C))
    for i in range(K):
        h0, h1 = _span(i, H, OH)
        for j in range(K):
            w0, w1 = _span(j, W, OW)
            xs = xq[:, :, h0 * STRIDE + i - PAD:(h1 - 1) * STRIDE + i - PAD + 1:STRIDE,
                    w0 * STRIDE + j - PAD:(w1 - 1) * STRIDE + j - PAD + 1:STRIDE]
            wq = mxq(wf[h0:h1, w0:w1, :, :, i, j], 3, "e4m3")
            acc[h0:h1, w0:w1] += xs.transpose(2, 3, 0, 1) @ wq.transpose(0, 1, 3, 2)
    return acc.transpose(2, 3, 0, 1) + f64(bias)[None]

@@ -1,0 +1,245 @@
+from contextlib import ExitStack
+
+import concourse.mybir as mybir
+from concourse.masks import make_identity
+
+BF16 = mybir.dt.bfloat16
+F32 = mybir.dt.float32
+U32 = mybir.dt.uint32
+U8 = mybir.dt.uint8
+FP8X4 = mybir.dt.float8_e4m3fn_x4
+
+P = 128
+B, C, O, H, W, KK = 512, 512, 128, 4, 4, 3
+S = H * W
+TAPS = KK * KK
+NBT = B // P
+UNIT = 512
+UW = 128
+RUN = 8
+
+N_VALID = 100
+FLOPS = 2 * B * O * C * N_VALID
+BYTES = B * C * S * 2 + N_VALID * O * C * 2 + O * S * 2 + B * O * S * 4
+
+XBUFS = 2
+WBUFS = 4
+SORT_ON_SCALAR = 4
+AHEAD = 2
+
+
+def valid_taps(h, w):
+    return [(i, j) for i in range(KK) for j in range(KK)
+            if 0 <= h + i - 1 < H and 0 <= w + j - 1 < W]
+
+
+def tile_locallyconnected2d_t_kernel(tc, x, weights, bias, out):
+    nc = tc.nc
+    x_rows = x.rearrange("(a p) c h w -> a p (c h w)", p=P)
+    w_rows = weights.rearrange("h w o c i j -> (h w) o (c i j)")
+    out_rows = out.rearrange("(t p) o h w -> t p (o h w)", p=P)
+    n_chunks = x_rows.shape[0]
+
+    with ExitStack() as ctx:
+        const = ctx.enter_context(tc.tile_pool(name="const", bufs=1))
+        xraw_pool = ctx.enter_context(tc.tile_pool(name="xraw", bufs=XBUFS))
+        wraw_pool = ctx.enter_context(tc.tile_pool(name="wraw", bufs=WBUFS))
+        work_pool = ctx.enter_context(tc.tile_pool(name="work", bufs=7))
+        wq_pool = ctx.enter_context(tc.tile_pool(name="wq", bufs=4))
+        tp_pool = ctx.enter_context(tc.psum_pool(name="tp", bufs=4))
+        acc_pool = ctx.enter_context(tc.psum_pool(name="acc", bufs=1))
+        ctx.enter_context(tc.manual_schedule())
+
+        ident = const.tile([P, P], F32, name="ident")
+        make_identity(nc, ident[:])
+        x_codes = const.tile([P, NBT * S * UW], U32, name="x_codes", align_bytes=64)
+        x_scales = const.tile([P, NBT * S * UW], U8, name="x_scales", align_bytes=64)
+        bias_sb = const.tile([P, O * S], BF16, name="bias_sb")
+        out_sb = [const.tile([P, O * S], F32, name="out_sb%d" % t) for t in range(NBT)]
+
+        state = {"xbank": 0, "sort": 0}
+
+        def quantise(codes, scales, stage, u0, n, c0):
+            nc.vector.quantize_mx(
+                out=codes[:, c0:c0 + n * UW].bitcast(FP8X4),
+                scales=scales[:, c0:c0 + n * UW],
+                in_=stage[:, u0 * UNIT:(u0 + n) * UNIT],
+            )
+
+        runs = []
+        for h in range(H):
+            row = []
+            for w in range(W):
+                taps = valid_taps(h, w)
+                for n, (i, j) in enumerate(taps):
+                    row.append((h, w, i, j, n == 0, n == len(taps) - 1))
+            if h == 0:
+                for w in range(W):
+                    runs.append((h, [u for u in row if u[1] == w]))
+            else:
+                for r0 in range(0, len(row), RUN):
+                    runs.append((h, row[r0:r0 + RUN]))
+        last_use = {}
+        for r, (h, units) in enumerate(runs):
+            for u in units:
+                last_use[u[0] * W + u[1]] = r
+
+        xraw = {}
+        wraw = {}
+
+        def load_x(a):
+            t = xraw_pool.tile([P, C * S], BF16, name="xraw%d" % a, tag="xraw")
+            nc.sync.dma_start(out=t[:], in_=x_rows[a])
+            xraw[a] = t
+
+        def load_w(g):
+            t = wraw_pool.tile([P, C * TAPS], BF16, name="wraw%d" % g, tag="wraw")
+            nc.sync.dma_start(out=t[:], in_=w_rows[g])
+            wraw[g] = t
+
+        sorted_w = {}
+
+        def sort_taps(r):
+            h, units = runs[r]
+            dst = work_pool.tile([P, RUN * UNIT], BF16, name="srt%d" % r, tag="work", align_bytes=64)
+            dst_v = dst.rearrange("p (k e m d) -> p e m d k", e=2, m=P, d=2)
+            k = 0
+            while k < len(units):
+                uh, uw, i, j = units[k][:4]
+                n = 1
+                while k + n < len(units) and units[k + n][:3] == (uh, uw, i):
+                    n += 1
+                src_v = wraw[uh * W + uw].rearrange("p (m e d t) -> p e m d t", e=2, d=2, t=TAPS)
+                t0 = i * KK + j
+                cnt = state["sort"]
+                state["sort"] = cnt + 1
+                for e in range(2):
+                    if cnt % SORT_ON_SCALAR == SORT_ON_SCALAR - 1:
+                        nc.scalar.copy(out=dst_v[:, e, :, :, k:k + n], in_=src_v[:, e, :, :, t0:t0 + n])
+                    else:
+                        nc.vector.tensor_copy(out=dst_v[:, e, :, :, k:k + n], in_=src_v[:, e, :, :, t0:t0 + n])
+                k += n
+            sorted_w[r] = dst
+            for g in range(S):
+                if last_use[g] == r and g + WBUFS < S:
+                    load_w(g + WBUFS)
+
+        for a in range(XBUFS):
+            load_x(a)
+
+        pending = []
+        xstage = {}
+        for a in range(n_chunks):
+            words = xraw[a].bitcast(F32).rearrange("p (m k) -> p m k", k=4 * S // 2)
+            for q in range(S // 2):
+                half, u0 = q // 4, (2 * q) % 8
+                if u0 == 0:
+                    xstage[half] = work_pool.tile([P, RUN * UNIT], BF16, name="xst%d_%d" % (a, half),
+                                                  tag="work", align_bytes=64)
+                bank = tp_pool.tile([P, UNIT], F32, name="xtp%d_%d" % (a, q), tag="tp")
+                for e in range(4):
+                    nc.tensor.transpose(bank[:, e * P:(e + 1) * P], words[:, :, (S // 2) * e + q], ident[:])
+                src = bank.bitcast(BF16).rearrange("p (e n g) -> p g n e", e=4, g=2)
+                dst = xstage[half].rearrange("p (u n e) -> p u n e", u=8, e=4)
+                k = state["xbank"]
+                state["xbank"] = k + 1
+                for g in range(2):
+                    if k % 3 == 1:
+                        nc.vector.tensor_copy(out=dst[:, u0 + g], in_=src[:, g])
+                    else:
+                        nc.scalar.copy(out=dst[:, u0 + g], in_=src[:, g])
+                if q == 3:
+                    for job in pending:
+                        quantise(*job)
+                    pending = []
+            for half in range(2):
+                pending.append((x_codes, x_scales, xstage[half], 0, 8, (a * S + 8 * half) * UW))
+            if a + XBUFS < n_chunks:
+                load_x(a + XBUFS)
+            elif a + XBUFS == n_chunks:
+                for g in range(WBUFS):
+                    load_w(g)
+                    if g == WBUFS - 1:
+                        nc.sync.dma_start(
+                            out=bias_sb[:],
+                            in_=bias.rearrange("o h w -> (o h w)").partition_broadcast(P))
+
+        sort_taps(0)
+        for job in pending:
+            quantise(*job)
+        sort_taps(1)
+
+        wq = {}
+        acc = {}
+
+        def transposes(r):
+            h, units = runs[r]
+            n = len(units)
+            stage = work_pool.tile([P, RUN * UNIT], BF16, name="wst%d" % r, tag="work", align_bytes=64)
+            words = sorted_w[r].bitcast(F32)
+            stage_w = stage.bitcast(F32)
+            for k in range(0, n, 2):
+                bank = tp_pool.tile([P, UNIT], F32, name="wtp%d_%d" % (r, k), tag="tp")
+                for e in range(4):
+                    c0 = (2 * k + e) * P
+                    nc.tensor.transpose(bank[:, e * P:(e + 1) * P], words[:, c0:c0 + P], ident[:])
+                nc.scalar.copy(
+                    out=stage_w[:, k * 256:(k + 2) * 256].rearrange("p (u o e) -> p u o e", u=2, e=2),
+                    in_=bank.rearrange("p (u e o) -> p u o e", u=2, e=2))
+            if r + AHEAD < len(runs):
+                sort_taps(r + AHEAD)
+            codes = wq_pool.tile([P, RUN * UW], U32, name="wc%d" % r, tag="wc", align_bytes=64)
+            scales = wq_pool.tile([P, RUN * UW], U8, name="ws%d" % r, tag="ws", align_bytes=64)
+            u0 = 0
+            for width in (8, 4, 2):
+                if n - u0 >= width:
+                    quantise(codes, scales, stage, u0, width, u0 * UW)
+                    u0 += width
+            wq[r] = (codes, scales)
+
+        def passes(h, bt, todo):
+            if (h, bt) not in acc:
+                acc[(h, bt)] = acc_pool.tile([P, W * O], F32, name="acc%d_%d" % (h, bt), tag="acc%d" % bt)
+            bank = acc[(h, bt)]
+            for r, k, (uh, uw, i, j, first, last) in todo:
+                codes, scales = wq[r]
+                s = (uh + i - 1) * W + (uw + j - 1)
+                xc = (bt * S + s) * UW
+                nc.tensor.matmul_mx(
+                    out=bank[:, uw * O:(uw + 1) * O],
+                    lhsT=x_codes[:, xc:xc + UW].bitcast(FP8X4),
+                    lhsT_scale=x_scales[:, xc:xc + UW],
+                    rhs=codes[:, k * UW:(k + 1) * UW].bitcast(FP8X4),
+                    rhs_scale=scales[:, k * UW:(k + 1) * UW],
+                    start=first,
+                    stop=last,
+                )
+
+        def finish(h, bt):
+            nc.vector.tensor_tensor(
+                out=out_sb[bt].rearrange("p (o s) -> p o s", s=S)[:, :, h * W:(h + 1) * W],
+                in0=acc[(h, bt)].rearrange("p (w o) -> p o w", w=W),
+                in1=bias_sb.rearrange("p (o s) -> p o s", s=S)[:, :, h * W:(h + 1) * W],
+                op=mybir.AluOpType.add,
+            )
+
+        def multiply(r):
+            h, units = runs[r]
+            closes = r + 1 == len(runs) or runs[r + 1][0] != h
+            todo = [(r, k, u) for k, u in enumerate(units)]
+            for bt in range(NBT):
+                passes(h, bt, todo)
+                if closes:
+                    finish(h, bt)
+
+        for r in range(len(runs)):
+            transposes(r)
+            if r >= 1 and runs[r - 1][0] != H - 1:
+                multiply(r - 1)
+
+        todo = [(r, k, u) for r in range(len(runs)) if runs[r][0] == H - 1
+                for k, u in enumerate(runs[r][1])]
+        for bt in range(NBT):
+            passes(H - 1, bt, todo)
+            finish(H - 1, bt)
+            nc.sync.dma_start(out=out_rows[bt], in_=out_sb[bt][:])

@@ -16,16 +16,19 @@ TAPS = KK * KK
 NBT = B // P
 UNIT = 512
 UW = 128
-RUN = 8
+MAXU = 9
 
 N_VALID = 100
 FLOPS = 2 * B * O * C * N_VALID
 BYTES = B * C * S * 2 + N_VALID * O * C * 2 + O * S * 2 + B * O * S * 4
 
-XBUFS = 2
-WBUFS = 4
-SORT_ON_SCALAR = 4
+WRAW_BUFS = 4
+XRAW_BUFS = 1
 AHEAD = 2
+X_BEFORE_LOC = {0: 0, 1: 3, 2: 6, 3: 16}
+X_JOB_PIXELS = {0: 8, 1: 8, 2: 8, 3: 4}
+BUSY = 1 << 20
+SORT_CYCLE = 4
 
 
 def valid_taps(h, w):
@@ -35,211 +38,210 @@ def valid_taps(h, w):
 
 def tile_locallyconnected2d_t_kernel(tc, x, weights, bias, out):
     nc = tc.nc
-    x_rows = x.rearrange("(a p) c h w -> a p (c h w)", p=P)
+    x_rows = x.rearrange("(t p) (z c) h w -> t z p (c h w)", p=P, z=2)
     w_rows = weights.rearrange("h w o c i j -> (h w) o (c i j)")
     out_rows = out.rearrange("(t p) o h w -> t p (o h w)", p=P)
-    n_chunks = x_rows.shape[0]
+
+    jobs = []
+    for loc in range(S + 1):
+        for bt in range(NBT):
+            if X_BEFORE_LOC[bt] == loc:
+                for s0 in range(0, S, X_JOB_PIXELS[bt]):
+                    jobs.append(("x", bt, s0))
+        if loc < S:
+            jobs.append(("w", loc, 0))
+    loads = []
+    for kind, n, s0 in jobs:
+        if kind == "w":
+            loads.append(("w", n, 0))
+        elif s0 == 0:
+            loads.append(("x", n, 0))
+            loads.append(("x", n, 1))
 
     with ExitStack() as ctx:
         const = ctx.enter_context(tc.tile_pool(name="const", bufs=1))
-        xraw_pool = ctx.enter_context(tc.tile_pool(name="xraw", bufs=XBUFS))
-        wraw_pool = ctx.enter_context(tc.tile_pool(name="wraw", bufs=WBUFS))
-        work_pool = ctx.enter_context(tc.tile_pool(name="work", bufs=7))
-        wq_pool = ctx.enter_context(tc.tile_pool(name="wq", bufs=4))
+        wraw_pool = ctx.enter_context(tc.tile_pool(name="wraw", bufs=WRAW_BUFS))
+        xraw_pool = ctx.enter_context(tc.tile_pool(name="xraw", bufs=XRAW_BUFS))
+        sort_pool = ctx.enter_context(tc.tile_pool(name="sort", bufs=3))
+        stage_pool = ctx.enter_context(tc.tile_pool(name="stage", bufs=2))
+        out_pool = ctx.enter_context(tc.tile_pool(name="outs", bufs=3))
         tp_pool = ctx.enter_context(tc.psum_pool(name="tp", bufs=4))
         acc_pool = ctx.enter_context(tc.psum_pool(name="acc", bufs=1))
         ctx.enter_context(tc.manual_schedule())
 
         ident = const.tile([P, P], F32, name="ident")
         make_identity(nc, ident[:])
-        x_codes = const.tile([P, NBT * S * UW], U32, name="x_codes", align_bytes=64)
-        x_scales = const.tile([P, NBT * S * UW], U8, name="x_scales", align_bytes=64)
         bias_sb = const.tile([P, O * S], BF16, name="bias_sb")
-        out_sb = [const.tile([P, O * S], F32, name="out_sb%d" % t) for t in range(NBT)]
 
-        state = {"xbank": 0, "sort": 0}
+        state = {"sort": 0, "time": 0, "evac": 0}
+        raw = {}
+        sorted_tiles = {}
+        stages = {}
+        operands = {}
+        acc = {}
+        unfinished = []
+        acc_free = {0: 0, 1: 1, 2: 2, 3: 3}
+        out_sb = {}
+        next_loc = [0] * NBT
 
-        def quantise(codes, scales, stage, u0, n, c0):
-            nc.vector.quantize_mx(
-                out=codes[:, c0:c0 + n * UW].bitcast(FP8X4),
-                scales=scales[:, c0:c0 + n * UW],
-                in_=stage[:, u0 * UNIT:(u0 + n) * UNIT],
-            )
+        def n_units(job):
+            return X_JOB_PIXELS[job[1]] if job[0] == "x" else len(valid_taps(job[1] // W, job[1] % W))
 
-        runs = []
-        for h in range(H):
-            row = []
-            for w in range(W):
-                taps = valid_taps(h, w)
-                for n, (i, j) in enumerate(taps):
-                    row.append((h, w, i, j, n == 0, n == len(taps) - 1))
-            if h == 0:
-                for w in range(W):
-                    runs.append((h, [u for u in row if u[1] == w]))
-            else:
-                for r0 in range(0, len(row), RUN):
-                    runs.append((h, row[r0:r0 + RUN]))
-        last_use = {}
-        for r, (h, units) in enumerate(runs):
-            for u in units:
-                last_use[u[0] * W + u[1]] = r
+        room = {"w": WRAW_BUFS, "x": 2 * XRAW_BUFS}
 
-        xraw = {}
-        wraw = {}
-
-        def load_x(a):
-            t = xraw_pool.tile([P, C * S], BF16, name="xraw%d" % a, tag="xraw")
-            nc.sync.dma_start(out=t[:], in_=x_rows[a])
-            xraw[a] = t
-
-        def load_w(g):
-            t = wraw_pool.tile([P, C * TAPS], BF16, name="wraw%d" % g, tag="wraw")
-            nc.sync.dma_start(out=t[:], in_=w_rows[g])
-            wraw[g] = t
-
-        sorted_w = {}
-
-        def sort_taps(r):
-            h, units = runs[r]
-            dst = work_pool.tile([P, RUN * UNIT], BF16, name="srt%d" % r, tag="work", align_bytes=64)
-            dst_v = dst.rearrange("p (k e m d) -> p e m d k", e=2, m=P, d=2)
-            k = 0
-            while k < len(units):
-                uh, uw, i, j = units[k][:4]
-                n = 1
-                while k + n < len(units) and units[k + n][:3] == (uh, uw, i):
-                    n += 1
-                src_v = wraw[uh * W + uw].rearrange("p (m e d t) -> p e m d t", e=2, d=2, t=TAPS)
-                t0 = i * KK + j
-                cnt = state["sort"]
-                state["sort"] = cnt + 1
-                for e in range(2):
-                    if cnt % SORT_ON_SCALAR == SORT_ON_SCALAR - 1:
-                        nc.scalar.copy(out=dst_v[:, e, :, :, k:k + n], in_=src_v[:, e, :, :, t0:t0 + n])
-                    else:
-                        nc.vector.tensor_copy(out=dst_v[:, e, :, :, k:k + n], in_=src_v[:, e, :, :, t0:t0 + n])
-                k += n
-            sorted_w[r] = dst
-            for g in range(S):
-                if last_use[g] == r and g + WBUFS < S:
-                    load_w(g + WBUFS)
-
-        for a in range(XBUFS):
-            load_x(a)
-
-        pending = []
-        xstage = {}
-        for a in range(n_chunks):
-            words = xraw[a].bitcast(F32).rearrange("p (m k) -> p m k", k=4 * S // 2)
-            for q in range(S // 2):
-                half, u0 = q // 4, (2 * q) % 8
-                if u0 == 0:
-                    xstage[half] = work_pool.tile([P, RUN * UNIT], BF16, name="xst%d_%d" % (a, half),
-                                                  tag="work", align_bytes=64)
-                bank = tp_pool.tile([P, UNIT], F32, name="xtp%d_%d" % (a, q), tag="tp")
-                for e in range(4):
-                    nc.tensor.transpose(bank[:, e * P:(e + 1) * P], words[:, :, (S // 2) * e + q], ident[:])
-                src = bank.bitcast(BF16).rearrange("p (e n g) -> p g n e", e=4, g=2)
-                dst = xstage[half].rearrange("p (u n e) -> p u n e", u=8, e=4)
-                k = state["xbank"]
-                state["xbank"] = k + 1
-                for g in range(2):
-                    if k % 3 == 1:
-                        nc.vector.tensor_copy(out=dst[:, u0 + g], in_=src[:, g])
-                    else:
-                        nc.scalar.copy(out=dst[:, u0 + g], in_=src[:, g])
-                if q == 3:
-                    for job in pending:
-                        quantise(*job)
-                    pending = []
-            for half in range(2):
-                pending.append((x_codes, x_scales, xstage[half], 0, 8, (a * S + 8 * half) * UW))
-            if a + XBUFS < n_chunks:
-                load_x(a + XBUFS)
-            elif a + XBUFS == n_chunks:
-                for g in range(WBUFS):
-                    load_w(g)
-                    if g == WBUFS - 1:
+        def load_more():
+            while loads and room[loads[0][0]] > 0:
+                kind, n, z = loads.pop(0)
+                room[kind] -= 1
+                if kind == "w":
+                    raw[("w", n)] = wraw_pool.tile([P, C * TAPS], BF16, name="raww%d" % n, tag="raww")
+                    nc.sync.dma_start(out=raw[("w", n)][:], in_=w_rows[n])
+                    if n == 1:
                         nc.sync.dma_start(
                             out=bias_sb[:],
                             in_=bias.rearrange("o h w -> (o h w)").partition_broadcast(P))
+                else:
+                    if z == 0:
+                        raw[("x", n)] = xraw_pool.tile([P, C * S], BF16, name="rawx%d" % n, tag="rawx")
+                    half = C * S // 2
+                    nc.sync.dma_start(out=raw[("x", n)][:, z * half:(z + 1) * half], in_=x_rows[n, z])
 
-        sort_taps(0)
-        for job in pending:
-            quantise(*job)
-        sort_taps(1)
+        def sort_copy(dst, src):
+            mine = []
+            for e in range(2):
+                cnt = state["sort"]
+                state["sort"] = cnt + 1
+                if cnt % SORT_CYCLE == SORT_CYCLE - 1:
+                    nc.scalar.copy(out=dst[:, e], in_=src[:, e])
+                else:
+                    mine.append(e)
+            if len(mine) == 2:
+                nc.vector.tensor_copy(out=dst, in_=src)
+            elif mine:
+                nc.vector.tensor_copy(out=dst[:, mine[0]], in_=src[:, mine[0]])
 
-        wq = {}
-        acc = {}
+        def sort(job):
+            kind, n, s0 = job
+            dst = sort_pool.tile([P, MAXU * UNIT], BF16, name="srt_%s%d_%d" % job, tag="srt", align_bytes=64)
+            if kind == "x":
+                dst_v = dst.rearrange("p (u e z m d) -> p z e m d u", e=2, z=2, d=2, u=MAXU)
+                for z in range(2):
+                    src_v = raw[("x", n)].rearrange("p (z m e d s) -> p z e m d s", z=2, e=2, d=2, s=S)[:, z]
+                    for u0 in range(0, n_units(job), 4):
+                        sort_copy(dst_v[:, z, :, :, :, u0:u0 + 4], src_v[:, :, :, :, s0 + u0:s0 + u0 + 4])
+                if s0 + n_units(job) == S:
+                    room["x"] += 2
+            else:
+                taps = valid_taps(n // W, n % W)
+                dst_v = dst.rearrange("p (k e m d) -> p e m d k", e=2, m=P, d=2)
+                src_v = raw[("w", n)].rearrange("p (m e d t) -> p e m d t", e=2, d=2, t=TAPS)
+                for i in range(KK):
+                    cols = [k for k, tap in enumerate(taps) if tap[0] == i]
+                    if cols:
+                        t0 = i * KK + taps[cols[0]][1]
+                        sort_copy(dst_v[:, :, :, :, cols[0]:cols[-1] + 1], src_v[:, :, :, :, t0:t0 + len(cols)])
+                room["w"] += 1
+            sorted_tiles[job] = dst
+            load_more()
 
-        def transposes(r):
-            h, units = runs[r]
-            n = len(units)
-            stage = work_pool.tile([P, RUN * UNIT], BF16, name="wst%d" % r, tag="work", align_bytes=64)
-            words = sorted_w[r].bitcast(F32)
+        def transposes(job):
+            n = n_units(job)
+            stage = stage_pool.tile([P, MAXU * UNIT], BF16, name="stg_%s%d_%d" % job, tag="stg", align_bytes=64)
+            stages[job] = stage
+            words = sorted_tiles[job].bitcast(F32)
             stage_w = stage.bitcast(F32)
             for k in range(0, n, 2):
-                bank = tp_pool.tile([P, UNIT], F32, name="wtp%d_%d" % (r, k), tag="tp")
-                for e in range(4):
+                m = min(2, n - k)
+                bank = tp_pool.tile([P, UNIT], F32, name="tp_%s%d_%d_%d" % (job + (k,)), tag="tp")
+                for e in range(2 * m):
                     c0 = (2 * k + e) * P
                     nc.tensor.transpose(bank[:, e * P:(e + 1) * P], words[:, c0:c0 + P], ident[:])
-                nc.scalar.copy(
-                    out=stage_w[:, k * 256:(k + 2) * 256].rearrange("p (u o e) -> p u o e", u=2, e=2),
-                    in_=bank.rearrange("p (u e o) -> p u o e", u=2, e=2))
-            if r + AHEAD < len(runs):
-                sort_taps(r + AHEAD)
-            codes = wq_pool.tile([P, RUN * UW], U32, name="wc%d" % r, tag="wc", align_bytes=64)
-            scales = wq_pool.tile([P, RUN * UW], U8, name="ws%d" % r, tag="ws", align_bytes=64)
+                dst = stage_w[:, k * 256:(k + m) * 256].rearrange("p (u o e) -> p u o e", u=m, e=2)
+                src = bank[:, :m * 256].rearrange("p (u e o) -> p u o e", u=m, e=2)
+                nc.scalar.copy(out=dst, in_=src)
+
+        def quantise(job):
+            n = n_units(job)
+            cw = const.tile([P, n * UW], U32, name="cod_%s%d_%d" % job, align_bytes=64)
+            sc = const.tile([P, n * UW], U8, name="scl_%s%d_%d" % job, align_bytes=64)
             u0 = 0
-            for width in (8, 4, 2):
+            for width in (8, 4, 2, 1):
                 if n - u0 >= width:
-                    quantise(codes, scales, stage, u0, width, u0 * UW)
+                    nc.vector.quantize_mx(
+                        out=cw[:, u0 * UW:(u0 + width) * UW].bitcast(FP8X4),
+                        scales=sc[:, u0 * UW:(u0 + width) * UW],
+                        in_=stages[job][:, u0 * UNIT:(u0 + width) * UNIT],
+                    )
                     u0 += width
-            wq[r] = (codes, scales)
+            for u in range(n):
+                operands[(job[0], job[1], job[2] + u)] = (cw, sc, u * UW)
 
-        def passes(h, bt, todo):
-            if (h, bt) not in acc:
-                acc[(h, bt)] = acc_pool.tile([P, W * O], F32, name="acc%d_%d" % (h, bt), tag="acc%d" % bt)
-            bank = acc[(h, bt)]
-            for r, k, (uh, uw, i, j, first, last) in todo:
-                codes, scales = wq[r]
-                s = (uh + i - 1) * W + (uw + j - 1)
-                xc = (bt * S + s) * UW
+        def passes_of(bt, loc):
+            h, w = loc // W, loc % W
+            return [(("x", bt, (h + i - 1) * W + w + j - 1), ("w", loc, k))
+                    for k, (i, j) in enumerate(valid_taps(h, w))]
+
+        def multiply(bt, loc):
+            h, w = loc // W, loc % W
+            if w == 0:
+                tag = min(acc_free, key=acc_free.get)
+                if acc_free[tag] == BUSY:
+                    finish_rows()
+                    tag = min(acc_free, key=acc_free.get)
+                acc_free[tag] = BUSY
+                acc[(bt, h)] = (tag, acc_pool.tile([P, W * O], F32, name="acc%d_%d" % (h, bt), tag="acc%d" % tag))
+            bank = acc[(bt, h)][1]
+            todo = passes_of(bt, loc)
+            for xj, wj in todo:
+                xc, xs, x0 = operands[xj]
+                wc, ws, w0 = operands[wj]
                 nc.tensor.matmul_mx(
-                    out=bank[:, uw * O:(uw + 1) * O],
-                    lhsT=x_codes[:, xc:xc + UW].bitcast(FP8X4),
-                    lhsT_scale=x_scales[:, xc:xc + UW],
-                    rhs=codes[:, k * UW:(k + 1) * UW].bitcast(FP8X4),
-                    rhs_scale=scales[:, k * UW:(k + 1) * UW],
-                    start=first,
-                    stop=last,
+                    out=bank[:, w * O:(w + 1) * O],
+                    lhsT=xc[:, x0:x0 + UW].bitcast(FP8X4),
+                    lhsT_scale=xs[:, x0:x0 + UW],
+                    rhs=wc[:, w0:w0 + UW].bitcast(FP8X4),
+                    rhs_scale=ws[:, w0:w0 + UW],
+                    start=wj == todo[0][1],
+                    stop=wj == todo[-1][1],
                 )
+            if w == W - 1:
+                unfinished.append((bt, h))
 
-        def finish(h, bt):
-            nc.vector.tensor_tensor(
-                out=out_sb[bt].rearrange("p (o s) -> p o s", s=S)[:, :, h * W:(h + 1) * W],
-                in0=acc[(h, bt)].rearrange("p (w o) -> p o w", w=W),
-                in1=bias_sb.rearrange("p (o s) -> p o s", s=S)[:, :, h * W:(h + 1) * W],
-                op=mybir.AluOpType.add,
-            )
+        def finish_rows():
+            while unfinished:
+                bt, h = unfinished.pop(0)
+                tag, bank = acc[(bt, h)]
+                if h == 0:
+                    out_sb[bt] = out_pool.tile([P, O * S], F32, name="out%d" % bt, tag="out")
+                nc.vector.tensor_tensor(
+                    out=out_sb[bt].rearrange("p (o s) -> p o s", s=S)[:, :, h * W:(h + 1) * W],
+                    in0=bank.rearrange("p (w o) -> p o w", w=W),
+                    in1=bias_sb.rearrange("p (o s) -> p o s", s=S)[:, :, h * W:(h + 1) * W],
+                    op=mybir.AluOpType.add,
+                )
+                state["time"] += 1
+                acc_free[tag] = 3 + state["time"]
+                if h == H - 1:
+                    nc.sync.dma_start(out=out_rows[bt], in_=out_sb[bt][:])
 
-        def multiply(r):
-            h, units = runs[r]
-            closes = r + 1 == len(runs) or runs[r + 1][0] != h
-            todo = [(r, k, u) for k, u in enumerate(units)]
-            for bt in range(NBT):
-                passes(h, bt, todo)
-                if closes:
-                    finish(h, bt)
+        def multiply_all():
+            for loc in range(S):
+                for bt in range(NBT):
+                    if next_loc[bt] == loc and all(
+                            xj in operands and wj in operands for xj, wj in passes_of(bt, loc)):
+                        multiply(bt, loc)
+                        next_loc[bt] += 1
 
-        for r in range(len(runs)):
-            transposes(r)
-            if r >= 1 and runs[r - 1][0] != H - 1:
-                multiply(r - 1)
-
-        todo = [(r, k, u) for r in range(len(runs)) if runs[r][0] == H - 1
-                for k, u in enumerate(runs[r][1])]
-        for bt in range(NBT):
-            passes(H - 1, bt, todo)
-            finish(H - 1, bt)
-            nc.sync.dma_start(out=out_rows[bt], in_=out_sb[bt][:])
+        load_more()
+        for job in jobs[:AHEAD]:
+            sort(job)
+        for n in range(len(jobs) + 1):
+            if n < len(jobs):
+                transposes(jobs[n])
+            if n >= 1:
+                quantise(jobs[n - 1])
+            finish_rows()
+            if n + AHEAD < len(jobs):
+                sort(jobs[n + AHEAD])
+            multiply_all()
+        finish_rows()

@@ -96,10 +96,6 @@ def tile_locallyconnected2d_t_kernel(tc, x, weights, bias, out):
                 if kind == "w":
                     raw[("w", n)] = wraw_pool.tile([P, C * TAPS], BF16, name="raww%d" % n, tag="raww")
                     nc.sync.dma_start(out=raw[("w", n)][:], in_=w_rows[n])
-                    if n == 1:
-                        nc.sync.dma_start(
-                            out=bias_sb[:],
-                            in_=bias.rearrange("o h w -> (o h w)").partition_broadcast(P))
                 else:
                     if z == 0:
                         raw[("x", n)] = xraw_pool.tile([P, C * S], BF16, name="rawx%d" % n, tag="rawx")
@@ -232,9 +228,20 @@ def tile_locallyconnected2d_t_kernel(tc, x, weights, bias, out):
                         multiply(bt, loc)
                         next_loc[bt] += 1
 
+        bias_row = const.tile([P, O * S], BF16, name="bias_row")
+        ones = const.tile([P, P], BF16, name="ones")
+        nc.vector.memset(bias_row[:], 0.0)
+        nc.vector.memset(ones[:], 1.0)
+        nc.scalar.dma_start(out=bias_row[0:1, :], in_=bias.rearrange("o h w -> (o h w)").unsqueeze(0))
+
         load_more()
         for job in jobs[:AHEAD]:
             sort(job)
+        for t in range(NBT):
+            bank = acc_pool.tile([P, W * O], F32, name="bias%d" % t, tag="acc%d" % t)
+            cols = slice(t * W * O, (t + 1) * W * O)
+            nc.tensor.matmul(bank[:], lhsT=ones[:], rhs=bias_row[:, cols], start=True, stop=True)
+            nc.scalar.copy(out=bias_sb[:, cols], in_=bank[:])
         for n in range(len(jobs) + 1):
             if n < len(jobs):
                 transposes(jobs[n])

@@ -22,10 +22,13 @@ N_VALID = 100
 FLOPS = 2 * B * O * C * N_VALID
 BYTES = B * C * S * 2 + N_VALID * O * C * 2 + O * S * 2 + B * O * S * 4
 
-WRAW_BUFS = 4
+WRAW_BUFS = 3
 XRAW_BUFS = 1
 AHEAD = 2
 X_BEFORE_LOC = {0: 0, 1: 3, 2: 6, 3: 16}
+X_LOADS = {0: 4, 1: 2, 2: 2, 3: 2}
+BIAS_STEP = 1
+QLAG = 2
 X_JOB_PIXELS = {0: 8, 1: 8, 2: 8, 3: 4}
 BUSY = 1 << 20
 SORT_CYCLE = 4
@@ -38,7 +41,7 @@ def valid_taps(h, w):
 
 def tile_locallyconnected2d_t_kernel(tc, x, weights, bias, out):
     nc = tc.nc
-    x_rows = x.rearrange("(t p) (z c) h w -> t z p (c h w)", p=P, z=2)
+    x_rows = x.rearrange("(t p) c h w -> t p (c h w)", p=P)
     w_rows = weights.rearrange("h w o c i j -> (h w) o (c i j)")
     out_rows = out.rearrange("(t p) o h w -> t p (o h w)", p=P)
 
@@ -55,15 +58,15 @@ def tile_locallyconnected2d_t_kernel(tc, x, weights, bias, out):
         if kind == "w":
             loads.append(("w", n, 0))
         elif s0 == 0:
-            loads.append(("x", n, 0))
-            loads.append(("x", n, 1))
+            for z in range(X_LOADS[n]):
+                loads.append(("x", n, z))
 
     with ExitStack() as ctx:
         const = ctx.enter_context(tc.tile_pool(name="const", bufs=1))
         wraw_pool = ctx.enter_context(tc.tile_pool(name="wraw", bufs=WRAW_BUFS))
         xraw_pool = ctx.enter_context(tc.tile_pool(name="xraw", bufs=XRAW_BUFS))
         sort_pool = ctx.enter_context(tc.tile_pool(name="sort", bufs=3))
-        stage_pool = ctx.enter_context(tc.tile_pool(name="stage", bufs=2))
+        stage_pool = ctx.enter_context(tc.tile_pool(name="stage", bufs=QLAG + 1))
         out_pool = ctx.enter_context(tc.tile_pool(name="outs", bufs=3))
         tp_pool = ctx.enter_context(tc.psum_pool(name="tp", bufs=4))
         acc_pool = ctx.enter_context(tc.psum_pool(name="acc", bufs=1))
@@ -75,6 +78,7 @@ def tile_locallyconnected2d_t_kernel(tc, x, weights, bias, out):
 
         state = {"sort": 0, "time": 0, "evac": 0}
         raw = {}
+        raw_x = {}
         sorted_tiles = {}
         stages = {}
         operands = {}
@@ -87,20 +91,22 @@ def tile_locallyconnected2d_t_kernel(tc, x, weights, bias, out):
         def n_units(job):
             return X_JOB_PIXELS[job[1]] if job[0] == "x" else len(valid_taps(job[1] // W, job[1] % W))
 
-        room = {"w": WRAW_BUFS, "x": 2 * XRAW_BUFS}
+        room = {"w": WRAW_BUFS, "x": XRAW_BUFS}
 
         def load_more():
-            while loads and room[loads[0][0]] > 0:
+            while loads and (room[loads[0][0]] > 0 or (loads[0][0] == "x" and loads[0][1] in raw_x)):
                 kind, n, z = loads.pop(0)
-                room[kind] -= 1
+                if kind == "w" or n not in raw_x:
+                    room[kind] -= 1
                 if kind == "w":
                     raw[("w", n)] = wraw_pool.tile([P, C * TAPS], BF16, name="raww%d" % n, tag="raww")
                     nc.sync.dma_start(out=raw[("w", n)][:], in_=w_rows[n])
                 else:
-                    if z == 0:
-                        raw[("x", n)] = xraw_pool.tile([P, C * S], BF16, name="rawx%d" % n, tag="rawx")
-                    half = C * S // 2
-                    nc.sync.dma_start(out=raw[("x", n)][:, z * half:(z + 1) * half], in_=x_rows[n, z])
+                    if n not in raw_x:
+                        raw_x[n] = xraw_pool.tile([P, C * S], BF16, name="rawx%d" % n, tag="rawx")
+                    size = C * S // X_LOADS[n]
+                    nc.sync.dma_start(out=raw_x[n][:, z * size:(z + 1) * size],
+                                      in_=x_rows[n][:, z * size:(z + 1) * size])
 
         def sort_copy(dst, src):
             mine = []
@@ -120,13 +126,14 @@ def tile_locallyconnected2d_t_kernel(tc, x, weights, bias, out):
             kind, n, s0 = job
             dst = sort_pool.tile([P, MAXU * UNIT], BF16, name="srt_%s%d_%d" % job, tag="srt", align_bytes=64)
             if kind == "x":
-                dst_v = dst.rearrange("p (u e z m d) -> p z e m d u", e=2, z=2, d=2, u=MAXU)
-                for z in range(2):
-                    src_v = raw[("x", n)].rearrange("p (z m e d s) -> p z e m d s", z=2, e=2, d=2, s=S)[:, z]
+                zs = X_LOADS[n]
+                dst_v = dst.rearrange("p (u e z m d) -> p z e m d u", e=2, z=zs, d=2, u=MAXU)
+                for z in range(zs):
+                    src_v = raw_x[n].rearrange("p (z m e d s) -> p z e m d s", z=zs, e=2, d=2, s=S)[:, z]
                     for u0 in range(0, n_units(job), 4):
                         sort_copy(dst_v[:, z, :, :, :, u0:u0 + 4], src_v[:, :, :, :, s0 + u0:s0 + u0 + 4])
                 if s0 + n_units(job) == S:
-                    room["x"] += 2
+                    room["x"] += 1
             else:
                 taps = valid_taps(n // W, n % W)
                 dst_v = dst.rearrange("p (k e m d) -> p e m d k", e=2, m=P, d=2)
@@ -230,25 +237,29 @@ def tile_locallyconnected2d_t_kernel(tc, x, weights, bias, out):
 
         bias_row = const.tile([P, O * S], BF16, name="bias_row")
         ones = const.tile([P, P], BF16, name="ones")
-        nc.vector.memset(bias_row[:], 0.0)
+        nc.vector.memset(bias_row[:].bitcast(U32), 0)
         nc.vector.memset(ones[:], 1.0)
         nc.scalar.dma_start(out=bias_row[0:1, :], in_=bias.rearrange("o h w -> (o h w)").unsqueeze(0))
+
+        def spread_bias():
+            for t in range(NBT):
+                bank = tp_pool.tile([P, UNIT], F32, name="bias%d" % t, tag="tp")
+                cols = slice(t * W * O, (t + 1) * W * O)
+                nc.tensor.matmul(bank[:], lhsT=ones[:], rhs=bias_row[:, cols], start=True, stop=True)
+                nc.scalar.copy(out=bias_sb[:, cols], in_=bank[:])
 
         load_more()
         for job in jobs[:AHEAD]:
             sort(job)
-        for t in range(NBT):
-            bank = acc_pool.tile([P, W * O], F32, name="bias%d" % t, tag="acc%d" % t)
-            cols = slice(t * W * O, (t + 1) * W * O)
-            nc.tensor.matmul(bank[:], lhsT=ones[:], rhs=bias_row[:, cols], start=True, stop=True)
-            nc.scalar.copy(out=bias_sb[:, cols], in_=bank[:])
-        for n in range(len(jobs) + 1):
+        for n in range(len(jobs) + QLAG):
             if n < len(jobs):
                 transposes(jobs[n])
-            if n >= 1:
-                quantise(jobs[n - 1])
+            if n >= QLAG:
+                quantise(jobs[n - QLAG])
             finish_rows()
             if n + AHEAD < len(jobs):
                 sort(jobs[n + AHEAD])
+            if n == BIAS_STEP:
+                spread_bias()
             multiply_all()
         finish_rows()

@@ -22,16 +22,19 @@ N_VALID = 100
 FLOPS = 2 * B * O * C * N_VALID
 BYTES = B * C * S * 2 + N_VALID * O * C * 2 + O * S * 2 + B * O * S * 4
 
-WRAW_BUFS = 3
+WRAW_BUFS = 4
 XRAW_BUFS = 1
 AHEAD = 2
-X_BEFORE_LOC = {0: 0, 1: 3, 2: 6, 3: 16}
+X_BEFORE_LOC = {0: 0, 1: 2, 2: 5, 3: 16}
 X_LOADS = {0: 4, 1: 2, 2: 2, 3: 2}
+X_LAST = [16, 16, 16, 16]
 BIAS_STEP = 1
+DIRECT_AT = {3: [9, 10, 11, 12]}
+DSPLIT = 64
 QLAG = 2
 X_JOB_PIXELS = {0: 8, 1: 8, 2: 8, 3: 4}
 BUSY = 1 << 20
-SORT_CYCLE = 4
+SORT_CYCLE = 5
 
 
 def valid_taps(h, w):
@@ -42,14 +45,15 @@ def valid_taps(h, w):
 def tile_locallyconnected2d_t_kernel(tc, x, weights, bias, out):
     nc = tc.nc
     x_rows = x.rearrange("(t p) c h w -> t p (c h w)", p=P)
+    x_quads = x.rearrange("(t b) (p j) h w -> t p b (j h w)", b=P, j=4)
     w_rows = weights.rearrange("h w o c i j -> (h w) o (c i j)")
     out_rows = out.rearrange("(t p) o h w -> t p (o h w)", p=P)
 
     jobs = []
     for loc in range(S + 1):
         for bt in range(NBT):
-            if X_BEFORE_LOC[bt] == loc:
-                for s0 in range(0, S, X_JOB_PIXELS[bt]):
+            for k, s0 in enumerate(range(0, S, X_JOB_PIXELS[bt])):
+                if (X_BEFORE_LOC[bt] if bt < 3 else X_LAST[k]) == loc:
                     jobs.append(("x", bt, s0))
         if loc < S:
             jobs.append(("w", loc, 0))
@@ -57,7 +61,9 @@ def tile_locallyconnected2d_t_kernel(tc, x, weights, bias, out):
     for kind, n, s0 in jobs:
         if kind == "w":
             loads.append(("w", n, 0))
-        elif s0 == 0:
+            for bt in DIRECT_AT:
+                loads += [("x", bt, z) for z in range(len(DIRECT_AT[bt])) if DIRECT_AT[bt][z] == n]
+        elif s0 == 0 and n not in DIRECT_AT:
             for z in range(X_LOADS[n]):
                 loads.append(("x", n, z))
 
@@ -67,7 +73,8 @@ def tile_locallyconnected2d_t_kernel(tc, x, weights, bias, out):
         xraw_pool = ctx.enter_context(tc.tile_pool(name="xraw", bufs=XRAW_BUFS))
         sort_pool = ctx.enter_context(tc.tile_pool(name="sort", bufs=3))
         stage_pool = ctx.enter_context(tc.tile_pool(name="stage", bufs=QLAG + 1))
-        out_pool = ctx.enter_context(tc.tile_pool(name="outs", bufs=3))
+        out_pool = ctx.enter_context(tc.tile_pool(name="outs", bufs=NBT - 1))
+        xcode_pool = ctx.enter_context(tc.tile_pool(name="xcodes", bufs=NBT))
         tp_pool = ctx.enter_context(tc.psum_pool(name="tp", bufs=4))
         acc_pool = ctx.enter_context(tc.psum_pool(name="acc", bufs=1))
         ctx.enter_context(tc.manual_schedule())
@@ -76,7 +83,7 @@ def tile_locallyconnected2d_t_kernel(tc, x, weights, bias, out):
         make_identity(nc, ident[:])
         bias_sb = const.tile([P, O * S], BF16, name="bias_sb")
 
-        state = {"sort": 0, "time": 0, "evac": 0}
+        state = {"sort": 0, "time": 0}
         raw = {}
         raw_x = {}
         sorted_tiles = {}
@@ -104,6 +111,12 @@ def tile_locallyconnected2d_t_kernel(tc, x, weights, bias, out):
                 else:
                     if n not in raw_x:
                         raw_x[n] = xraw_pool.tile([P, C * S], BF16, name="rawx%d" % n, tag="rawx")
+                    if n in DIRECT_AT:
+                        size = P // len(DIRECT_AT[n])
+                        nc.sync.dma_start(
+                            out=raw_x[n].rearrange("p (b e) -> p b e", b=P)[:, z * size:(z + 1) * size],
+                            in_=x_quads[n][:, z * size:(z + 1) * size])
+                        continue
                     size = C * S // X_LOADS[n]
                     nc.sync.dma_start(out=raw_x[n][:, z * size:(z + 1) * size],
                                       in_=x_rows[n][:, z * size:(z + 1) * size])
@@ -125,7 +138,15 @@ def tile_locallyconnected2d_t_kernel(tc, x, weights, bias, out):
         def sort(job):
             kind, n, s0 = job
             dst = sort_pool.tile([P, MAXU * UNIT], BF16, name="srt_%s%d_%d" % job, tag="srt", align_bytes=64)
-            if kind == "x":
+            if kind == "x" and n in DIRECT_AT:
+                dst_v = dst.rearrange("p (u b j) -> p b j u", u=MAXU, j=4)
+                src_v = raw_x[n].rearrange("p (b j s) -> p b j s", j=4, s=S)
+                for u0 in range(0, n_units(job), 4):
+                    nc.scalar.copy(out=dst_v[:, DSPLIT:, :, u0:u0 + 4], in_=src_v[:, DSPLIT:, :, s0 + u0:s0 + u0 + 4])
+                    nc.vector.tensor_copy(out=dst_v[:, :DSPLIT, :, u0:u0 + 4], in_=src_v[:, :DSPLIT, :, s0 + u0:s0 + u0 + 4])
+                if s0 + n_units(job) == S:
+                    room["x"] += 1
+            elif kind == "x":
                 zs = X_LOADS[n]
                 dst_v = dst.rearrange("p (u e z m d) -> p z e m d u", e=2, z=zs, d=2, u=MAXU)
                 for z in range(zs):
@@ -147,8 +168,13 @@ def tile_locallyconnected2d_t_kernel(tc, x, weights, bias, out):
             sorted_tiles[job] = dst
             load_more()
 
+        def direct(job):
+            return job[0] == "x" and job[1] in DIRECT_AT
+
         def transposes(job):
             n = n_units(job)
+            if direct(job):
+                return
             stage = stage_pool.tile([P, MAXU * UNIT], BF16, name="stg_%s%d_%d" % job, tag="stg", align_bytes=64)
             stages[job] = stage
             words = sorted_tiles[job].bitcast(F32)
@@ -165,19 +191,29 @@ def tile_locallyconnected2d_t_kernel(tc, x, weights, bias, out):
 
         def quantise(job):
             n = n_units(job)
-            cw = const.tile([P, n * UW], U32, name="cod_%s%d_%d" % job, align_bytes=64)
-            sc = const.tile([P, n * UW], U8, name="scl_%s%d_%d" % job, align_bytes=64)
+            stage = sorted_tiles[job] if direct(job) else stages[job]
+            kind, number, s0 = job
+            half = s0 // (S // 2)
+            if kind == "w":
+                cw = const.tile([P, n * UW], U32, name="cod_w%d" % number, align_bytes=64)
+                sc = const.tile([P, n * UW], U8, name="scl_w%d" % number, align_bytes=64)
+            elif s0 % (S // 2) == 0:
+                cw = xcode_pool.tile([P, S // 2 * UW], U32, name="cod_x%d_%d" % (number, half), tag="xc%d" % half, align_bytes=64)
+                sc = xcode_pool.tile([P, S // 2 * UW], U8, name="scl_x%d_%d" % (number, half), tag="xs%d" % half, align_bytes=64)
+            else:
+                cw, sc, base = operands[(kind, number, half * S // 2)]
+            first = s0 % (S // 2) if kind == "x" else 0
             u0 = 0
             for width in (8, 4, 2, 1):
                 if n - u0 >= width:
                     nc.vector.quantize_mx(
-                        out=cw[:, u0 * UW:(u0 + width) * UW].bitcast(FP8X4),
-                        scales=sc[:, u0 * UW:(u0 + width) * UW],
-                        in_=stages[job][:, u0 * UNIT:(u0 + width) * UNIT],
+                        out=cw[:, (first + u0) * UW:(first + u0 + width) * UW].bitcast(FP8X4),
+                        scales=sc[:, (first + u0) * UW:(first + u0 + width) * UW],
+                        in_=stage[:, u0 * UNIT:(u0 + width) * UNIT],
                     )
                     u0 += width
             for u in range(n):
-                operands[(job[0], job[1], job[2] + u)] = (cw, sc, u * UW)
+                operands[(kind, number, s0 + u)] = (cw, sc, (first + u) * UW)
 
         def passes_of(bt, loc):
             h, w = loc // W, loc % W
@@ -215,7 +251,10 @@ def tile_locallyconnected2d_t_kernel(tc, x, weights, bias, out):
                 bt, h = unfinished.pop(0)
                 tag, bank = acc[(bt, h)]
                 if h == 0:
-                    out_sb[bt] = out_pool.tile([P, O * S], F32, name="out%d" % bt, tag="out")
+                    if bt == NBT - 1:
+                        out_sb[bt] = wraw_pool.tile([P, C * TAPS // 2], F32, name="out%d" % bt, tag="raww")[:, :O * S]
+                    else:
+                        out_sb[bt] = out_pool.tile([P, O * S], F32, name="out%d" % bt, tag="out")
                 nc.vector.tensor_tensor(
                     out=out_sb[bt].rearrange("p (o s) -> p o s", s=S)[:, :, h * W:(h + 1) * W],
                     in0=bank.rearrange("p (w o) -> p o w", w=W),
@@ -225,7 +264,7 @@ def tile_locallyconnected2d_t_kernel(tc, x, weights, bias, out):
                 state["time"] += 1
                 acc_free[tag] = 3 + state["time"]
                 if h == H - 1:
-                    nc.sync.dma_start(out=out_rows[bt], in_=out_sb[bt][:])
+                    nc.sync.dma_start(out=out_rows[bt], in_=out_sb[bt][:, :])
 
         def multiply_all():
             for loc in range(S):
@@ -235,9 +274,9 @@ def tile_locallyconnected2d_t_kernel(tc, x, weights, bias, out):
                         multiply(bt, loc)
                         next_loc[bt] += 1
 
-        bias_row = const.tile([P, O * S], BF16, name="bias_row")
+        bias_row = stage_pool.tile([P, MAXU * UNIT], BF16, name="bias_row", tag="stg", align_bytes=64)[:, :O * S]
         ones = const.tile([P, P], BF16, name="ones")
-        nc.vector.memset(bias_row[:].bitcast(U32), 0)
+        nc.vector.memset(bias_row.bitcast(U32), 0)
         nc.vector.memset(ones[:], 1.0)
         nc.scalar.dma_start(out=bias_row[0:1, :], in_=bias.rearrange("o h w -> (o h w)").unsqueeze(0))
 
@@ -254,8 +293,10 @@ def tile_locallyconnected2d_t_kernel(tc, x, weights, bias, out):
         for n in range(len(jobs) + QLAG):
             if n < len(jobs):
                 transposes(jobs[n])
-            if n >= QLAG:
+            if n >= QLAG and not direct(jobs[n - QLAG]):
                 quantise(jobs[n - QLAG])
+            if n < len(jobs) and direct(jobs[n]):
+                quantise(jobs[n])
             finish_rows()
             if n + AHEAD < len(jobs):
                 sort(jobs[n + AHEAD])

@@ -34,7 +34,7 @@ DSPLIT = 64
 QLAG = 2
 X_JOB_PIXELS = {0: 8, 1: 8, 2: 8, 3: 4}
 BUSY = 1 << 20
-SORT_CYCLE = 5
+SHARED_ROWS = 2
 
 
 def valid_taps(h, w):
@@ -83,7 +83,7 @@ def tile_locallyconnected2d_t_kernel(tc, x, weights, bias, out):
         make_identity(nc, ident[:])
         bias_sb = const.tile([P, O * S], BF16, name="bias_sb")
 
-        state = {"sort": 0, "time": 0}
+        state = {"time": 0}
         raw = {}
         raw_x = {}
         sorted_tiles = {}
@@ -121,19 +121,12 @@ def tile_locallyconnected2d_t_kernel(tc, x, weights, bias, out):
                     nc.sync.dma_start(out=raw_x[n][:, z * size:(z + 1) * size],
                                       in_=x_rows[n][:, z * size:(z + 1) * size])
 
-        def sort_copy(dst, src):
-            mine = []
-            for e in range(2):
-                cnt = state["sort"]
-                state["sort"] = cnt + 1
-                if cnt % SORT_CYCLE == SORT_CYCLE - 1:
-                    nc.scalar.copy(out=dst[:, e], in_=src[:, e])
-                else:
-                    mine.append(e)
-            if len(mine) == 2:
+        def sort_copy(dst, src, shared):
+            if shared:
+                nc.scalar.copy(out=dst[:, 1], in_=src[:, 1])
+                nc.vector.tensor_copy(out=dst[:, 0], in_=src[:, 0])
+            else:
                 nc.vector.tensor_copy(out=dst, in_=src)
-            elif mine:
-                nc.vector.tensor_copy(out=dst[:, mine[0]], in_=src[:, mine[0]])
 
         def sort(job):
             kind, n, s0 = job
@@ -152,7 +145,7 @@ def tile_locallyconnected2d_t_kernel(tc, x, weights, bias, out):
                 for z in range(zs):
                     src_v = raw_x[n].rearrange("p (z m e d s) -> p z e m d s", z=zs, e=2, d=2, s=S)[:, z]
                     for u0 in range(0, n_units(job), 4):
-                        sort_copy(dst_v[:, z, :, :, :, u0:u0 + 4], src_v[:, :, :, :, s0 + u0:s0 + u0 + 4])
+                        sort_copy(dst_v[:, z, :, :, :, u0:u0 + 4], src_v[:, :, :, :, s0 + u0:s0 + u0 + 4], (z * 2 + u0 // 4) % 2 == 1)
                 if s0 + n_units(job) == S:
                     room["x"] += 1
             else:
@@ -163,7 +156,7 @@ def tile_locallyconnected2d_t_kernel(tc, x, weights, bias, out):
                     cols = [k for k, tap in enumerate(taps) if tap[0] == i]
                     if cols:
                         t0 = i * KK + taps[cols[0]][1]
-                        sort_copy(dst_v[:, :, :, :, cols[0]:cols[-1] + 1], src_v[:, :, :, :, t0:t0 + len(cols)])
+                        sort_copy(dst_v[:, :, :, :, cols[0]:cols[-1] + 1], src_v[:, :, :, :, t0:t0 + len(cols)], i < SHARED_ROWS and len(taps) > 4)
                 room["w"] += 1
             sorted_tiles[job] = dst
             load_more()
@@ -281,11 +274,12 @@ def tile_locallyconnected2d_t_kernel(tc, x, weights, bias, out):
         nc.scalar.dma_start(out=bias_row[0:1, :], in_=bias.rearrange("o h w -> (o h w)").unsqueeze(0))
 
         def spread_bias():
-            for t in range(NBT):
-                bank = tp_pool.tile([P, UNIT], F32, name="bias%d" % t, tag="tp")
-                cols = slice(t * W * O, (t + 1) * W * O)
-                nc.tensor.matmul(bank[:], lhsT=ones[:], rhs=bias_row[:, cols], start=True, stop=True)
-                nc.scalar.copy(out=bias_sb[:, cols], in_=bank[:])
+            for t in range(2):
+                bank = tp_pool.tile([P, 2 * UNIT], BF16, name="bias%d" % t, tag="tp")
+                for k in range(2):
+                    nc.tensor.matmul(bank[:, k * UNIT:(k + 1) * UNIT], lhsT=ones[:],
+                                     rhs=bias_row[:, (2 * t + k) * UNIT:(2 * t + k + 1) * UNIT], start=True, stop=True)
+                nc.scalar.copy(out=bias_sb[:, 2 * t * UNIT:2 * (t + 1) * UNIT], in_=bank[:])
 
         load_more()
         for job in jobs[:AHEAD]:

@@ -29,12 +29,11 @@ X_BEFORE_LOC = {0: 0, 1: 2, 2: 5, 3: 16}
 X_LOADS = {0: 4, 1: 2, 2: 2, 3: 2}
 X_LAST = [16, 16, 16, 16]
 BIAS_STEP = 1
-DIRECT_AT = {3: [9, 10, 11, 12]}
+DIRECT_AT = {3: [13, 14, 15, 15]}
 DSPLIT = 64
 QLAG = 2
 X_JOB_PIXELS = {0: 8, 1: 8, 2: 8, 3: 4}
 BUSY = 1 << 20
-SHARED_ROWS = 2
 
 
 def valid_taps(h, w):
@@ -81,7 +80,7 @@ def tile_locallyconnected2d_t_kernel(tc, x, weights, bias, out):
 
         ident = const.tile([P, P], F32, name="ident")
         make_identity(nc, ident[:])
-        bias_sb = const.tile([P, O * S], BF16, name="bias_sb")
+        bias_sb = const.tile([P, H * O * W], BF16, name="bias_sb")
 
         state = {"time": 0}
         raw = {}
@@ -145,7 +144,7 @@ def tile_locallyconnected2d_t_kernel(tc, x, weights, bias, out):
                 for z in range(zs):
                     src_v = raw_x[n].rearrange("p (z m e d s) -> p z e m d s", z=zs, e=2, d=2, s=S)[:, z]
                     for u0 in range(0, n_units(job), 4):
-                        sort_copy(dst_v[:, z, :, :, :, u0:u0 + 4], src_v[:, :, :, :, s0 + u0:s0 + u0 + 4], (z * 2 + u0 // 4) % 2 == 1)
+                        sort_copy(dst_v[:, z, :, :, :, u0:u0 + 4], src_v[:, :, :, :, s0 + u0:s0 + u0 + 4], (z * 2 + u0 // 4) % 4 == 1)
                 if s0 + n_units(job) == S:
                     room["x"] += 1
             else:
@@ -156,7 +155,7 @@ def tile_locallyconnected2d_t_kernel(tc, x, weights, bias, out):
                     cols = [k for k, tap in enumerate(taps) if tap[0] == i]
                     if cols:
                         t0 = i * KK + taps[cols[0]][1]
-                        sort_copy(dst_v[:, :, :, :, cols[0]:cols[-1] + 1], src_v[:, :, :, :, t0:t0 + len(cols)], i < SHARED_ROWS and len(taps) > 4)
+                        sort_copy(dst_v[:, :, :, :, cols[0]:cols[-1] + 1], src_v[:, :, :, :, t0:t0 + len(cols)], i == 1 or (i == 0 and len(taps) == TAPS))
                 room["w"] += 1
             sorted_tiles[job] = dst
             load_more()
@@ -251,7 +250,7 @@ def tile_locallyconnected2d_t_kernel(tc, x, weights, bias, out):
                 nc.vector.tensor_tensor(
                     out=out_sb[bt].rearrange("p (o s) -> p o s", s=S)[:, :, h * W:(h + 1) * W],
                     in0=bank.rearrange("p (w o) -> p o w", w=W),
-                    in1=bias_sb.rearrange("p (o s) -> p o s", s=S)[:, :, h * W:(h + 1) * W],
+                    in1=bias_sb[:, h * W * O:(h + 1) * W * O].rearrange("p (o w) -> p o w", w=W),
                     op=mybir.AluOpType.add,
                 )
                 state["time"] += 1
@@ -260,8 +259,8 @@ def tile_locallyconnected2d_t_kernel(tc, x, weights, bias, out):
                     nc.sync.dma_start(out=out_rows[bt], in_=out_sb[bt][:, :])
 
         def multiply_all():
-            for loc in range(S):
-                for bt in range(NBT):
+            for loc, bt in ([(loc, bt) for loc in range(S) for bt in range(NBT - 1)]
+                            + [(loc, NBT - 1) for loc in range(S)]):
                     if next_loc[bt] == loc and all(
                             xj in operands and wj in operands for xj, wj in passes_of(bt, loc)):
                         multiply(bt, loc)
@@ -277,8 +276,10 @@ def tile_locallyconnected2d_t_kernel(tc, x, weights, bias, out):
             for t in range(2):
                 bank = tp_pool.tile([P, 2 * UNIT], BF16, name="bias%d" % t, tag="tp")
                 for k in range(2):
+                    h = 2 * t + k
                     nc.tensor.matmul(bank[:, k * UNIT:(k + 1) * UNIT], lhsT=ones[:],
-                                     rhs=bias_row[:, (2 * t + k) * UNIT:(2 * t + k + 1) * UNIT], start=True, stop=True)
+                                     rhs=bias_row.rearrange("p (o h w) -> p h o w", h=H, w=W)[:, h],
+                                     start=True, stop=True)
                 nc.scalar.copy(out=bias_sb[:, 2 * t * UNIT:2 * (t + 1) * UNIT], in_=bank[:])
 
         load_more()

@@ -25,12 +25,10 @@ BYTES = B * C * S * 2 + N_VALID * O * C * 2 + O * S * 2 + B * O * S * 4
 WRAW_BUFS = 4
 XRAW_BUFS = 1
 AHEAD = 2
-X_BEFORE_LOC = {0: 0, 1: 2, 2: 5, 3: 16}
+X_BEFORE_LOC = {0: 0, 1: 3, 2: 6, 3: 16}
 X_LOADS = {0: 4, 1: 2, 2: 2, 3: 2}
-X_LAST = [16, 16, 16, 16]
+X_LAST = [14, 15, 16, 16]
 BIAS_STEP = 1
-DIRECT_AT = {3: [13, 14, 15, 15]}
-DSPLIT = 64
 QLAG = 2
 X_JOB_PIXELS = {0: 8, 1: 8, 2: 8, 3: 4}
 BUSY = 1 << 20
@@ -44,7 +42,6 @@ def valid_taps(h, w):
 def tile_locallyconnected2d_t_kernel(tc, x, weights, bias, out):
     nc = tc.nc
     x_rows = x.rearrange("(t p) c h w -> t p (c h w)", p=P)
-    x_quads = x.rearrange("(t b) (p j) h w -> t p b (j h w)", b=P, j=4)
     w_rows = weights.rearrange("h w o c i j -> (h w) o (c i j)")
     out_rows = out.rearrange("(t p) o h w -> t p (o h w)", p=P)
 
@@ -60,9 +57,7 @@ def tile_locallyconnected2d_t_kernel(tc, x, weights, bias, out):
     for kind, n, s0 in jobs:
         if kind == "w":
             loads.append(("w", n, 0))
-            for bt in DIRECT_AT:
-                loads += [("x", bt, z) for z in range(len(DIRECT_AT[bt])) if DIRECT_AT[bt][z] == n]
-        elif s0 == 0 and n not in DIRECT_AT:
+        elif s0 == 0:
             for z in range(X_LOADS[n]):
                 loads.append(("x", n, z))
 
@@ -110,12 +105,6 @@ def tile_locallyconnected2d_t_kernel(tc, x, weights, bias, out):
                 else:
                     if n not in raw_x:
                         raw_x[n] = xraw_pool.tile([P, C * S], BF16, name="rawx%d" % n, tag="rawx")
-                    if n in DIRECT_AT:
-                        size = P // len(DIRECT_AT[n])
-                        nc.sync.dma_start(
-                            out=raw_x[n].rearrange("p (b e) -> p b e", b=P)[:, z * size:(z + 1) * size],
-                            in_=x_quads[n][:, z * size:(z + 1) * size])
-                        continue
                     size = C * S // X_LOADS[n]
                     nc.sync.dma_start(out=raw_x[n][:, z * size:(z + 1) * size],
                                       in_=x_rows[n][:, z * size:(z + 1) * size])
@@ -130,15 +119,7 @@ def tile_locallyconnected2d_t_kernel(tc, x, weights, bias, out):
         def sort(job):
             kind, n, s0 = job
             dst = sort_pool.tile([P, MAXU * UNIT], BF16, name="srt_%s%d_%d" % job, tag="srt", align_bytes=64)
-            if kind == "x" and n in DIRECT_AT:
-                dst_v = dst.rearrange("p (u b j) -> p b j u", u=MAXU, j=4)
-                src_v = raw_x[n].rearrange("p (b j s) -> p b j s", j=4, s=S)
-                for u0 in range(0, n_units(job), 4):
-                    nc.scalar.copy(out=dst_v[:, DSPLIT:, :, u0:u0 + 4], in_=src_v[:, DSPLIT:, :, s0 + u0:s0 + u0 + 4])
-                    nc.vector.tensor_copy(out=dst_v[:, :DSPLIT, :, u0:u0 + 4], in_=src_v[:, :DSPLIT, :, s0 + u0:s0 + u0 + 4])
-                if s0 + n_units(job) == S:
-                    room["x"] += 1
-            elif kind == "x":
+            if kind == "x":
                 zs = X_LOADS[n]
                 dst_v = dst.rearrange("p (u e z m d) -> p z e m d u", e=2, z=zs, d=2, u=MAXU)
                 for z in range(zs):
@@ -160,13 +141,8 @@ def tile_locallyconnected2d_t_kernel(tc, x, weights, bias, out):
             sorted_tiles[job] = dst
             load_more()
 
-        def direct(job):
-            return job[0] == "x" and job[1] in DIRECT_AT
-
         def transposes(job):
             n = n_units(job)
-            if direct(job):
-                return
             stage = stage_pool.tile([P, MAXU * UNIT], BF16, name="stg_%s%d_%d" % job, tag="stg", align_bytes=64)
             stages[job] = stage
             words = sorted_tiles[job].bitcast(F32)
@@ -183,7 +159,7 @@ def tile_locallyconnected2d_t_kernel(tc, x, weights, bias, out):
 
         def quantise(job):
             n = n_units(job)
-            stage = sorted_tiles[job] if direct(job) else stages[job]
+            stage = stages[job]
             kind, number, s0 = job
             half = s0 // (S // 2)
             if kind == "w":
@@ -288,10 +264,8 @@ def tile_locallyconnected2d_t_kernel(tc, x, weights, bias, out):
         for n in range(len(jobs) + QLAG):
             if n < len(jobs):
                 transposes(jobs[n])
-            if n >= QLAG and not direct(jobs[n - QLAG]):
+            if n >= QLAG:
                 quantise(jobs[n - QLAG])
-            if n < len(jobs) and direct(jobs[n]):
-                quantise(jobs[n])
             finish_rows()
             if n + AHEAD < len(jobs):
                 sort(jobs[n + AHEAD])

@@ -25,11 +25,13 @@ BYTES = B * C * S * 2 + N_VALID * O * C * 2 + O * S * 2 + B * O * S * 4
 WRAW_BUFS = 4
 XRAW_BUFS = 1
 AHEAD = 2
-X_BEFORE_LOC = {0: 0, 1: 3, 2: 6, 3: 16}
+X_BEFORE_LOC = {0: 0, 1: 2, 2: 5, 3: 16}
 X_LOADS = {0: 4, 1: 2, 2: 2, 3: 2}
-X_LAST = [14, 15, 16, 16]
+X_LAST = [15, 16, 16, 16]
 BIAS_STEP = 1
+ROW_ORDER = (0, 1, 2, 3)
 QLAG = 2
+SORT_CYCLE = 4
 X_JOB_PIXELS = {0: 8, 1: 8, 2: 8, 3: 4}
 BUSY = 1 << 20
 
@@ -46,13 +48,14 @@ def tile_locallyconnected2d_t_kernel(tc, x, weights, bias, out):
     out_rows = out.rearrange("(t p) o h w -> t p (o h w)", p=P)
 
     jobs = []
-    for loc in range(S + 1):
+    locs = [h * W + w for h in ROW_ORDER for w in range(W)]
+    for step in range(S + 1):
         for bt in range(NBT):
             for k, s0 in enumerate(range(0, S, X_JOB_PIXELS[bt])):
-                if (X_BEFORE_LOC[bt] if bt < 3 else X_LAST[k]) == loc:
+                if (X_BEFORE_LOC[bt] if bt < 3 else X_LAST[k]) == step:
                     jobs.append(("x", bt, s0))
-        if loc < S:
-            jobs.append(("w", loc, 0))
+        if step < S:
+            jobs.append(("w", locs[step], 0))
     loads = []
     for kind, n, s0 in jobs:
         if kind == "w":
@@ -77,7 +80,7 @@ def tile_locallyconnected2d_t_kernel(tc, x, weights, bias, out):
         make_identity(nc, ident[:])
         bias_sb = const.tile([P, H * O * W], BF16, name="bias_sb")
 
-        state = {"time": 0}
+        state = {"time": 0, "half": 0}
         raw = {}
         raw_x = {}
         sorted_tiles = {}
@@ -109,23 +112,43 @@ def tile_locallyconnected2d_t_kernel(tc, x, weights, bias, out):
                     nc.sync.dma_start(out=raw_x[n][:, z * size:(z + 1) * size],
                                       in_=x_rows[n][:, z * size:(z + 1) * size])
 
-        def sort_copy(dst, src, shared):
-            if shared:
-                nc.scalar.copy(out=dst[:, 1], in_=src[:, 1])
-                nc.vector.tensor_copy(out=dst[:, 0], in_=src[:, 0])
-            else:
+        def sort_copy(dst, src):
+            mine = []
+            for e in range(2):
+                state["half"] += 1
+                if state["half"] % SORT_CYCLE == 0:
+                    nc.scalar.copy(out=dst[:, e], in_=src[:, e])
+                else:
+                    mine.append(e)
+            if len(mine) == 2:
                 nc.vector.tensor_copy(out=dst, in_=src)
+            elif mine:
+                nc.vector.tensor_copy(out=dst[:, mine[0]], in_=src[:, mine[0]])
+
+        def sort_pixels(job, dst, pieces):
+            kind, n, s0 = job
+            zs = X_LOADS[n]
+            dst_v = dst.rearrange("p (u e z m d) -> p z e m d u", e=2, z=zs, d=2, u=MAXU)
+            for z in pieces:
+                src_v = raw_x[n].rearrange("p (z m e d s) -> p z e m d s", z=zs, e=2, d=2, s=S)[:, z]
+                for u0 in range(0, n_units(job), 4):
+                    sort_copy(dst_v[:, z, :, :, :, u0:u0 + 4], src_v[:, :, :, :, s0 + u0:s0 + u0 + 4])
+
+        def sort_first(first_jobs):
+            for job in first_jobs:
+                sorted_tiles[job] = sort_pool.tile([P, MAXU * UNIT], BF16, name="srt_%s%d_%d" % job, tag="srt",
+                                                   align_bytes=64)
+            for z in range(X_LOADS[0]):
+                for job in first_jobs:
+                    sort_pixels(job, sorted_tiles[job], [z])
+            room["x"] += 1
+            load_more()
 
         def sort(job):
             kind, n, s0 = job
             dst = sort_pool.tile([P, MAXU * UNIT], BF16, name="srt_%s%d_%d" % job, tag="srt", align_bytes=64)
             if kind == "x":
-                zs = X_LOADS[n]
-                dst_v = dst.rearrange("p (u e z m d) -> p z e m d u", e=2, z=zs, d=2, u=MAXU)
-                for z in range(zs):
-                    src_v = raw_x[n].rearrange("p (z m e d s) -> p z e m d s", z=zs, e=2, d=2, s=S)[:, z]
-                    for u0 in range(0, n_units(job), 4):
-                        sort_copy(dst_v[:, z, :, :, :, u0:u0 + 4], src_v[:, :, :, :, s0 + u0:s0 + u0 + 4], (z * 2 + u0 // 4) % 4 == 1)
+                sort_pixels(job, dst, range(X_LOADS[n]))
                 if s0 + n_units(job) == S:
                     room["x"] += 1
             else:
@@ -136,7 +159,7 @@ def tile_locallyconnected2d_t_kernel(tc, x, weights, bias, out):
                     cols = [k for k, tap in enumerate(taps) if tap[0] == i]
                     if cols:
                         t0 = i * KK + taps[cols[0]][1]
-                        sort_copy(dst_v[:, :, :, :, cols[0]:cols[-1] + 1], src_v[:, :, :, :, t0:t0 + len(cols)], i == 1 or (i == 0 and len(taps) == TAPS))
+                        sort_copy(dst_v[:, :, :, :, cols[0]:cols[-1] + 1], src_v[:, :, :, :, t0:t0 + len(cols)])
                 room["w"] += 1
             sorted_tiles[job] = dst
             load_more()
@@ -218,7 +241,7 @@ def tile_locallyconnected2d_t_kernel(tc, x, weights, bias, out):
             while unfinished:
                 bt, h = unfinished.pop(0)
                 tag, bank = acc[(bt, h)]
-                if h == 0:
+                if h == ROW_ORDER[0]:
                     if bt == NBT - 1:
                         out_sb[bt] = wraw_pool.tile([P, C * TAPS // 2], F32, name="out%d" % bt, tag="raww")[:, :O * S]
                     else:
@@ -231,16 +254,16 @@ def tile_locallyconnected2d_t_kernel(tc, x, weights, bias, out):
                 )
                 state["time"] += 1
                 acc_free[tag] = 3 + state["time"]
-                if h == H - 1:
+                if h == ROW_ORDER[-1]:
                     nc.sync.dma_start(out=out_rows[bt], in_=out_sb[bt][:, :])
 
         def multiply_all():
-            for loc, bt in ([(loc, bt) for loc in range(S) for bt in range(NBT - 1)]
-                            + [(loc, NBT - 1) for loc in range(S)]):
-                    if next_loc[bt] == loc and all(
-                            xj in operands and wj in operands for xj, wj in passes_of(bt, loc)):
-                        multiply(bt, loc)
-                        next_loc[bt] += 1
+            for k, bt in ([(k, bt) for k in range(S) for bt in range(NBT - 1)]
+                          + [(k, NBT - 1) for k in range(S)]):
+                if next_loc[bt] == k and all(
+                        xj in operands and wj in operands for xj, wj in passes_of(bt, locs[k])):
+                    multiply(bt, locs[k])
+                    next_loc[bt] += 1
 
         bias_row = stage_pool.tile([P, MAXU * UNIT], BF16, name="bias_row", tag="stg", align_bytes=64)[:, :O * S]
         ones = const.tile([P, P], BF16, name="ones")
@@ -259,8 +282,7 @@ def tile_locallyconnected2d_t_kernel(tc, x, weights, bias, out):
                 nc.scalar.copy(out=bias_sb[:, 2 * t * UNIT:2 * (t + 1) * UNIT], in_=bank[:])
 
         load_more()
-        for job in jobs[:AHEAD]:
-            sort(job)
+        sort_first(jobs[:AHEAD])
         for n in range(len(jobs) + QLAG):
             if n < len(jobs):
                 transposes(jobs[n])

@@ -31,6 +31,7 @@ X_LAST = [15, 16, 16, 16]
 BIAS_STEP = 1
 ROW_ORDER = (0, 1, 2, 3)
 QLAG = 2
+EARLY = 2
 SORT_CYCLE = 4
 X_JOB_PIXELS = {0: 8, 1: 8, 2: 8, 3: 4}
 BUSY = 1 << 20
@@ -80,7 +81,7 @@ def tile_locallyconnected2d_t_kernel(tc, x, weights, bias, out):
         make_identity(nc, ident[:])
         bias_sb = const.tile([P, H * O * W], BF16, name="bias_sb")
 
-        state = {"time": 0, "half": 0}
+        state = {"quantised": 0, "time": 0, "half": 0}
         raw = {}
         raw_x = {}
         sorted_tiles = {}
@@ -178,7 +179,10 @@ def tile_locallyconnected2d_t_kernel(tc, x, weights, bias, out):
                     nc.tensor.transpose(bank[:, e * P:(e + 1) * P], words[:, c0:c0 + P], ident[:])
                 dst = stage_w[:, k * 256:(k + m) * 256].rearrange("p (u o e) -> p u o e", u=m, e=2)
                 src = bank[:, :m * 256].rearrange("p (u e o) -> p u o e", u=m, e=2)
-                nc.scalar.copy(out=dst, in_=src)
+                if job == jobs[0] and k // 2 % 2 == 1:
+                    nc.vector.tensor_copy(out=dst, in_=src)
+                else:
+                    nc.scalar.copy(out=dst, in_=src)
 
         def quantise(job):
             n = n_units(job)
@@ -286,11 +290,12 @@ def tile_locallyconnected2d_t_kernel(tc, x, weights, bias, out):
         for n in range(len(jobs) + QLAG):
             if n < len(jobs):
                 transposes(jobs[n])
-            if n >= QLAG:
-                quantise(jobs[n - QLAG])
-            finish_rows()
+            while state["quantised"] < n - (QLAG if n > EARLY else 1) + 1 and state["quantised"] < len(jobs):
+                quantise(jobs[state["quantised"]])
+                state["quantised"] += 1
             if n + AHEAD < len(jobs):
                 sort(jobs[n + AHEAD])
+            finish_rows()
             if n == BIAS_STEP:
                 spread_bias()
             multiply_all()

from contextlib import ExitStack

import concourse.mybir as mybir
from concourse.masks import make_identity

BF16 = mybir.dt.bfloat16
F32 = mybir.dt.float32
U32 = mybir.dt.uint32
U8 = mybir.dt.uint8
FP8X4 = mybir.dt.float8_e4m3fn_x4

P = 128
B, C, O, H, W, KK = 512, 512, 128, 4, 4, 3
S = H * W
TAPS = KK * KK
NBT = B // P
UNIT = 512
UW = 128
MAXU = 9

N_VALID = 100
FLOPS = 2 * B * O * C * N_VALID
BYTES = B * C * S * 2 + N_VALID * O * C * 2 + O * S * 2 + B * O * S * 4

WRAW_BUFS = 4
XRAW_BUFS = 1
AHEAD = 2
X_BEFORE_LOC = {0: 0, 1: 2, 2: 5, 3: 16}
X_LOADS = {0: 4, 1: 2, 2: 2, 3: 2}
X_LAST = [15, 16, 16, 16]
BIAS_STEP = 1
ROW_ORDER = (0, 1, 2, 3)
QLAG = 2
EARLY = 2
SORT_CYCLE = 4
X_JOB_PIXELS = {0: 8, 1: 8, 2: 8, 3: 4}
BUSY = 1 << 20


def valid_taps(h, w):
    return [(i, j) for i in range(KK) for j in range(KK)
            if 0 <= h + i - 1 < H and 0 <= w + j - 1 < W]


def tile_locallyconnected2d_t_kernel(tc, x, weights, bias, out):
    nc = tc.nc
    x_rows = x.rearrange("(t p) c h w -> t p (c h w)", p=P)
    w_rows = weights.rearrange("h w o c i j -> (h w) o (c i j)")
    out_rows = out.rearrange("(t p) o h w -> t p (o h w)", p=P)

    jobs = []
    locs = [h * W + w for h in ROW_ORDER for w in range(W)]
    for step in range(S + 1):
        for bt in range(NBT):
            for k, s0 in enumerate(range(0, S, X_JOB_PIXELS[bt])):
                if (X_BEFORE_LOC[bt] if bt < 3 else X_LAST[k]) == step:
                    jobs.append(("x", bt, s0))
        if step < S:
            jobs.append(("w", locs[step], 0))
    loads = []
    for kind, n, s0 in jobs:
        if kind == "w":
            loads.append(("w", n, 0))
        elif s0 == 0:
            for z in range(X_LOADS[n]):
                loads.append(("x", n, z))

    with ExitStack() as ctx:
        const = ctx.enter_context(tc.tile_pool(name="const", bufs=1))
        wraw_pool = ctx.enter_context(tc.tile_pool(name="wraw", bufs=WRAW_BUFS))
        xraw_pool = ctx.enter_context(tc.tile_pool(name="xraw", bufs=XRAW_BUFS))
        sort_pool = ctx.enter_context(tc.tile_pool(name="sort", bufs=3))
        stage_pool = ctx.enter_context(tc.tile_pool(name="stage", bufs=QLAG + 1))
        out_pool = ctx.enter_context(tc.tile_pool(name="outs", bufs=NBT - 1))
        xcode_pool = ctx.enter_context(tc.tile_pool(name="xcodes", bufs=NBT))
        tp_pool = ctx.enter_context(tc.psum_pool(name="tp", bufs=4))
        acc_pool = ctx.enter_context(tc.psum_pool(name="acc", bufs=1))
        ctx.enter_context(tc.manual_schedule())

        ident = const.tile([P, P], F32, name="ident")
        make_identity(nc, ident[:])
        bias_sb = const.tile([P, H * O * W], BF16, name="bias_sb")

        state = {"quantised": 0, "time": 0, "half": 0}
        raw = {}
        raw_x = {}
        sorted_tiles = {}
        stages = {}
        operands = {}
        acc = {}
        unfinished = []
        acc_free = {0: 0, 1: 1, 2: 2, 3: 3}
        out_sb = {}
        next_loc = [0] * NBT

        def n_units(job):
            return X_JOB_PIXELS[job[1]] if job[0] == "x" else len(valid_taps(job[1] // W, job[1] % W))

        room = {"w": WRAW_BUFS, "x": XRAW_BUFS}

        def load_more():
            while loads and (room[loads[0][0]] > 0 or (loads[0][0] == "x" and loads[0][1] in raw_x)):
                kind, n, z = loads.pop(0)
                if kind == "w" or n not in raw_x:
                    room[kind] -= 1
                if kind == "w":
                    raw[("w", n)] = wraw_pool.tile([P, C * TAPS], BF16, name="raww%d" % n, tag="raww")
                    nc.sync.dma_start(out=raw[("w", n)][:], in_=w_rows[n])
                else:
                    if n not in raw_x:
                        raw_x[n] = xraw_pool.tile([P, C * S], BF16, name="rawx%d" % n, tag="rawx")
                    size = C * S // X_LOADS[n]
                    nc.sync.dma_start(out=raw_x[n][:, z * size:(z + 1) * size],
                                      in_=x_rows[n][:, z * size:(z + 1) * size])

        def sort_copy(dst, src):
            mine = []
            for e in range(2):
                state["half"] += 1
                if state["half"] % SORT_CYCLE == 0:
                    nc.scalar.copy(out=dst[:, e], in_=src[:, e])
                else:
                    mine.append(e)
            if len(mine) == 2:
                nc.vector.tensor_copy(out=dst, in_=src)
            elif mine:
                nc.vector.tensor_copy(out=dst[:, mine[0]], in_=src[:, mine[0]])

        def sort_pixels(job, dst, pieces):
            kind, n, s0 = job
            zs = X_LOADS[n]
            dst_v = dst.rearrange("p (u e z m d) -> p z e m d u", e=2, z=zs, d=2, u=MAXU)
            for z in pieces:
                src_v = raw_x[n].rearrange("p (z m e d s) -> p z e m d s", z=zs, e=2, d=2, s=S)[:, z]
                for u0 in range(0, n_units(job), 4):
                    sort_copy(dst_v[:, z, :, :, :, u0:u0 + 4], src_v[:, :, :, :, s0 + u0:s0 + u0 + 4])

        def sort_first(first_jobs):
            for job in first_jobs:
                sorted_tiles[job] = sort_pool.tile([P, MAXU * UNIT], BF16, name="srt_%s%d_%d" % job, tag="srt",
                                                   align_bytes=64)
            for z in range(X_LOADS[0]):
                for job in first_jobs:
                    sort_pixels(job, sorted_tiles[job], [z])
            room["x"] += 1
            load_more()

        def sort(job):
            kind, n, s0 = job
            dst = sort_pool.tile([P, MAXU * UNIT], BF16, name="srt_%s%d_%d" % job, tag="srt", align_bytes=64)
            if kind == "x":
                sort_pixels(job, dst, range(X_LOADS[n]))
                if s0 + n_units(job) == S:
                    room["x"] += 1
            else:
                taps = valid_taps(n // W, n % W)
                dst_v = dst.rearrange("p (k e m d) -> p e m d k", e=2, m=P, d=2)
                src_v = raw[("w", n)].rearrange("p (m e d t) -> p e m d t", e=2, d=2, t=TAPS)
                for i in range(KK):
                    cols = [k for k, tap in enumerate(taps) if tap[0] == i]
                    if cols:
                        t0 = i * KK + taps[cols[0]][1]
                        sort_copy(dst_v[:, :, :, :, cols[0]:cols[-1] + 1], src_v[:, :, :, :, t0:t0 + len(cols)])
                room["w"] += 1
            sorted_tiles[job] = dst
            load_more()

        def transposes(job):
            n = n_units(job)
            stage = stage_pool.tile([P, MAXU * UNIT], BF16, name="stg_%s%d_%d" % job, tag="stg", align_bytes=64)
            stages[job] = stage
            words = sorted_tiles[job].bitcast(F32)
            stage_w = stage.bitcast(F32)
            for k in range(0, n, 2):
                m = min(2, n - k)
                bank = tp_pool.tile([P, UNIT], F32, name="tp_%s%d_%d_%d" % (job + (k,)), tag="tp")
                for e in range(2 * m):
                    c0 = (2 * k + e) * P
                    nc.tensor.transpose(bank[:, e * P:(e + 1) * P], words[:, c0:c0 + P], ident[:])
                dst = stage_w[:, k * 256:(k + m) * 256].rearrange("p (u o e) -> p u o e", u=m, e=2)
                src = bank[:, :m * 256].rearrange("p (u e o) -> p u o e", u=m, e=2)
                if job == jobs[0] and k // 2 % 2 == 1:
                    nc.vector.tensor_copy(out=dst, in_=src)
                else:
                    nc.scalar.copy(out=dst, in_=src)

        def quantise(job):
            n = n_units(job)
            stage = stages[job]
            kind, number, s0 = job
            half = s0 // (S // 2)
            if kind == "w":
                cw = const.tile([P, n * UW], U32, name="cod_w%d" % number, align_bytes=64)
                sc = const.tile([P, n * UW], U8, name="scl_w%d" % number, align_bytes=64)
            elif s0 % (S // 2) == 0:
                cw = xcode_pool.tile([P, S // 2 * UW], U32, name="cod_x%d_%d" % (number, half), tag="xc%d" % half, align_bytes=64)
                sc = xcode_pool.tile([P, S // 2 * UW], U8, name="scl_x%d_%d" % (number, half), tag="xs%d" % half, align_bytes=64)
            else:
                cw, sc, base = operands[(kind, number, half * S // 2)]
            first = s0 % (S // 2) if kind == "x" else 0
            u0 = 0
            for width in (8, 4, 2, 1):
                if n - u0 >= width:
                    nc.vector.quantize_mx(
                        out=cw[:, (first + u0) * UW:(first + u0 + width) * UW].bitcast(FP8X4),
                        scales=sc[:, (first + u0) * UW:(first + u0 + width) * UW],
                        in_=stage[:, u0 * UNIT:(u0 + width) * UNIT],
                    )
                    u0 += width
            for u in range(n):
                operands[(kind, number, s0 + u)] = (cw, sc, (first + u) * UW)

        def passes_of(bt, loc):
            h, w = loc // W, loc % W
            return [(("x", bt, (h + i - 1) * W + w + j - 1), ("w", loc, k))
                    for k, (i, j) in enumerate(valid_taps(h, w))]

        def multiply(bt, loc):
            h, w = loc // W, loc % W
            if w == 0:
                tag = min(acc_free, key=acc_free.get)
                if acc_free[tag] == BUSY:
                    finish_rows()
                    tag = min(acc_free, key=acc_free.get)
                acc_free[tag] = BUSY
                acc[(bt, h)] = (tag, acc_pool.tile([P, W * O], F32, name="acc%d_%d" % (h, bt), tag="acc%d" % tag))
            bank = acc[(bt, h)][1]
            todo = passes_of(bt, loc)
            for xj, wj in todo:
                xc, xs, x0 = operands[xj]
                wc, ws, w0 = operands[wj]
                nc.tensor.matmul_mx(
                    out=bank[:, w * O:(w + 1) * O],
                    lhsT=xc[:, x0:x0 + UW].bitcast(FP8X4),
                    lhsT_scale=xs[:, x0:x0 + UW],
                    rhs=wc[:, w0:w0 + UW].bitcast(FP8X4),
                    rhs_scale=ws[:, w0:w0 + UW],
                    start=wj == todo[0][1],
                    stop=wj == todo[-1][1],
                )
            if w == W - 1:
                unfinished.append((bt, h))

        def finish_rows():
            while unfinished:
                bt, h = unfinished.pop(0)
                tag, bank = acc[(bt, h)]
                if h == ROW_ORDER[0]:
                    if bt == NBT - 1:
                        out_sb[bt] = wraw_pool.tile([P, C * TAPS // 2], F32, name="out%d" % bt, tag="raww")[:, :O * S]
                    else:
                        out_sb[bt] = out_pool.tile([P, O * S], F32, name="out%d" % bt, tag="out")
                nc.vector.tensor_tensor(
                    out=out_sb[bt].rearrange("p (o s) -> p o s", s=S)[:, :, h * W:(h + 1) * W],
                    in0=bank.rearrange("p (w o) -> p o w", w=W),
                    in1=bias_sb[:, h * W * O:(h + 1) * W * O].rearrange("p (o w) -> p o w", w=W),
                    op=mybir.AluOpType.add,
                )
                state["time"] += 1
                acc_free[tag] = 3 + state["time"]
                if h == ROW_ORDER[-1]:
                    nc.sync.dma_start(out=out_rows[bt], in_=out_sb[bt][:, :])

        def multiply_all():
            for k, bt in ([(k, bt) for k in range(S) for bt in range(NBT - 1)]
                          + [(k, NBT - 1) for k in range(S)]):
                if next_loc[bt] == k and all(
                        xj in operands and wj in operands for xj, wj in passes_of(bt, locs[k])):
                    multiply(bt, locs[k])
                    next_loc[bt] += 1

        bias_row = stage_pool.tile([P, MAXU * UNIT], BF16, name="bias_row", tag="stg", align_bytes=64)[:, :O * S]
        ones = const.tile([P, P], BF16, name="ones")
        nc.vector.memset(bias_row.bitcast(U32), 0)
        nc.vector.memset(ones[:], 1.0)
        nc.scalar.dma_start(out=bias_row[0:1, :], in_=bias.rearrange("o h w -> (o h w)").unsqueeze(0))

        def spread_bias():
            for t in range(2):
                bank = tp_pool.tile([P, 2 * UNIT], BF16, name="bias%d" % t, tag="tp")
                for k in range(2):
                    h = 2 * t + k
                    nc.tensor.matmul(bank[:, k * UNIT:(k + 1) * UNIT], lhsT=ones[:],
                                     rhs=bias_row.rearrange("p (o h w) -> p h o w", h=H, w=W)[:, h],
                                     start=True, stop=True)
                nc.scalar.copy(out=bias_sb[:, 2 * t * UNIT:2 * (t + 1) * UNIT], in_=bank[:])

        load_more()
        sort_first(jobs[:AHEAD])
        for n in range(len(jobs) + QLAG):
            if n < len(jobs):
                transposes(jobs[n])
            while state["quantised"] < n - (QLAG if n > EARLY else 1) + 1 and state["quantised"] < len(jobs):
                quantise(jobs[state["quantised"]])
                state["quantised"] += 1
            if n + AHEAD < len(jobs):
                sort(jobs[n + AHEAD])
            finish_rows()
            if n == BIAS_STEP:
                spread_bias()
            multiply_all()
        finish_rows()
